import numpy as np
import ml_dtypes

BF16 = ml_dtypes.bfloat16


def bf(x):
    return np.asarray(x, np.float32).astype(BF16)


def f32(x):
    return np.asarray(x, np.float32)


def f64(x):
    return np.asarray(x).astype(np.float64)


def striped(idx):
    return np.tile(idx.reshape(-1, 16).T, (8, 1))


FN, FE, H, S, K, N, HALF, RUNS = 128, 1024, 512, 1024, 2, 2048, 512, 4


def setup_inputs():
    x = bf(np.random.standard_normal((FN, S)))
    ea = bf(np.random.standard_normal((FE, N)))
    w_node = bf(np.random.standard_normal((FN, H)) / np.sqrt(FN))
    w_edge = bf(np.random.standard_normal((FE, H)) / np.sqrt(FE))
    b_edge = f32(0.2 * np.random.standard_normal((H, 1)))
    w_m1 = bf(np.random.standard_normal((H + H + H, H)) / np.sqrt(H + H + H))
    b_m1 = f32(0.2 * np.random.standard_normal((H, 1)))
    w_m2 = bf(np.random.standard_normal((H, H)) / np.sqrt(H))
    b_m2 = f32(0.2 * np.random.standard_normal((H, 1)))
    idx = np.concatenate([np.random.permutation(S)[:HALF] for _ in range(RUNS)])
    return {"x": x, "ea": ea, "w_node": w_node, "w_edge": w_edge, "b_edge": b_edge, "w_m1": w_m1, "b_m1": b_m1, "w_m2": w_m2, "b_m2": b_m2, "offs": striped(idx)}


def reference(x, ea, w_node, w_edge, b_edge, w_m1, b_m1, w_m2, b_m2, offs):
    idx = offs[:16].T.reshape(-1)
    xs = f64(x)
    wn = f64(w_node)
    w1 = f64(w_m1)
    h = wn.T @ xs
    hs = wn.T @ xs[:, idx]
    e = f64(w_edge).T @ f64(ea) + f64(b_edge)
    u = np.repeat(w1[:H].T @ h, K, axis=1) + w1[H:H + H].T @ hs + w1[H + H:].T @ e + f64(b_m1)
    msg = f64(w_m2).T @ np.maximum(u, 0.0) + f64(b_m2)
    return h + msg.reshape(H, S, K).sum(axis=2)

@@ -1,0 +1,153 @@
+import concourse.mybir as mybir
+
+BF16, F32, U16 = mybir.dt.bfloat16, mybir.dt.float32, mybir.dt.uint16
+ADD = mybir.AluOpType.add
+IDENTITY = mybir.ActivationFunctionType.Identity
+RELU = mybir.ActivationFunctionType.Relu
+
+P = 128
+FN, FE, H = 128, 1024, 512
+S, N = 1024, 2048
+DEG = N // S
+COLS = 512
+HB = H // P
+EB = FE // P
+NODES = COLS // DEG
+PSUM_BANKS = 8
+
+FLOPS = 2 * (FN * H * S + FN * H * N + FE * H * N + H * H * S + 2 * H * H * N + H * H * N)
+
+
+def block(b):
+    return slice(b * P, (b + 1) * P)
+
+
+def chunk(i, width=COLS):
+    return slice(i * width, (i + 1) * width)
+
+
+def tile_messagepassing_b_kernel(
+    tc, x, ea, w_node, w_edge, b_edge, w_m1, b_m1, w_m2, b_m2, offs, out
+):
+    nc = tc.nc
+    with (
+        tc.tile_pool(name="held", bufs=1) as held,
+        tc.tile_pool(name="ring", bufs=4) as ring,
+        tc.psum_pool(name="psum", bufs=PSUM_BANKS) as psum,
+    ):
+        x_sb = held.tile([P, S], BF16, name="x_sb")
+        nc.sync.dma_start(x_sb[:], x)
+        w_node_sb = held.tile([P, H], BF16, name="w_node_sb")
+        nc.scalar.dma_start(w_node_sb[:], w_node)
+        offsets = held.tile([P, N // 16], U16, name="offsets")
+        nc.sync.dma_start(offsets[:], offs)
+
+        w_m1_blocks = w_m1.rearrange("(part d p) c -> part p d c", part=3, p=P)
+        w1_target = held.tile([P, HB, H], BF16, name="w1_target")
+        nc.sync.dma_start(w1_target[:], w_m1_blocks[0])
+        w_edge_sb = held.tile([P, EB, H], BF16, name="w_edge_sb")
+        nc.sync.dma_start(w_edge_sb[:], w_edge.rearrange("(q p) c -> p q c", p=P))
+        ea_sb = held.tile([P, EB, N], BF16, name="ea_sb")
+        for q in range(EB):
+            nc.sync.dma_start(ea_sb[:, q, :], ea[block(q), :])
+        w1_source = held.tile([P, HB, H], BF16, name="w1_source")
+        nc.sync.dma_start(w1_source[:], w_m1_blocks[1])
+        w1_edge = held.tile([P, HB, H], BF16, name="w1_edge")
+        nc.sync.dma_start(w1_edge[:], w_m1_blocks[2])
+        w_m2_sb = held.tile([P, HB, H], BF16, name="w_m2_sb")
+        nc.sync.dma_start(w_m2_sb[:], w_m2.rearrange("(d p) c -> p d c", p=P))
+
+        b_m1_sb = held.tile([P, HB], F32, name="b_m1_sb")
+        b_edge_sb = held.tile([P, HB], F32, name="b_edge_sb")
+        b_m2_sb = held.tile([P, HB], F32, name="b_m2_sb")
+        with nc.allow_non_contiguous_dma(reason="a bias has one 4-byte value for each partition"):
+            for bias_sb, bias in ((b_m1_sb, b_m1), (b_edge_sb, b_edge), (b_m2_sb, b_m2)):
+                nc.gpsimd.dma_start(bias_sb[:], bias.rearrange("(m p) o -> p (m o)", p=P))
+        b_out = held.tile([P, HB], F32, name="b_out")
+        nc.vector.tensor_scalar_mul(b_out[:], b_m2_sb[:], float(DEG))
+
+        h_f32 = held.tile([P, HB, S], F32, name="h_f32")
+        h_bf = held.tile([P, HB, S], BF16, name="h_bf")
+        hs_bf = held.tile([P, HB, N], BF16, name="hs_bf")
+        target = held.tile([P, HB, S], F32, name="target")
+        e_bf = held.tile([P, HB, N], BF16, name="e_bf")
+        relu_bf = [held.tile([P, HB, DEG, COLS], BF16, name=f"relu_bf{g}") for g in range(S // COLS)]
+
+        for g in range(S // COLS):
+            for m in range(HB):
+                h_ps = psum.tile([P, COLS], F32, tag="bank")
+                nc.tensor.matmul(h_ps[:], w_node_sb[:, block(m)], x_sb[:, chunk(g)])
+                if m % 2 == 0:
+                    nc.vector.tensor_copy(h_f32[:, m, chunk(g)], h_ps[:])
+                else:
+                    nc.scalar.copy(h_f32[:, m, chunk(g)], h_ps[:])
+                nc.gpsimd.tensor_copy(h_bf[:, m, chunk(g)], h_f32[:, m, chunk(g)])
+
+        for g in range(N // COLS):
+            looked_up = x_sb[:].indirect(offsets[:, chunk(g, COLS // 16)])
+            for m in range(HB):
+                hs_ps = psum.tile([P, COLS], F32, tag="bank")
+                nc.tensor.matmul(hs_ps[:], w_node_sb[:, block(m)], looked_up)
+                if m % 2 == 0:
+                    nc.vector.tensor_copy(hs_bf[:, m, chunk(g)], hs_ps[:])
+                else:
+                    nc.scalar.copy(hs_bf[:, m, chunk(g)], hs_ps[:])
+
+        for g in range(S // COLS):
+            for m in range(HB):
+                target_ps = psum.tile([P, COLS], F32, tag="bank")
+                for d in range(HB):
+                    nc.tensor.matmul(
+                        target_ps[:], w1_target[:, d, block(m)], h_bf[:, d, chunk(g)],
+                        start=(d == 0), stop=(d == HB - 1),
+                    )
+                nc.vector.tensor_scalar_add(target[:, m, chunk(g)], target_ps[:], b_m1_sb[:, m : m + 1])
+
+        for g in range(N // COLS):
+            for m in range(HB):
+                e_ps = psum.tile([P, COLS], F32, tag="bank")
+                for q in range(EB):
+                    nc.tensor.matmul(
+                        e_ps[:], w_edge_sb[:, q, block(m)], ea_sb[:, q, chunk(g)],
+                        start=(q == 0), stop=(q == EB - 1),
+                    )
+                nc.scalar.activation(e_bf[:, m, chunk(g)], e_ps[:], IDENTITY, bias=b_edge_sb[:, m : m + 1])
+
+        for g in range(N // COLS):
+            for m in range(HB):
+                u_ps = psum.tile([P, COLS], F32, tag="bank")
+                for d in range(HB):
+                    nc.tensor.matmul(
+                        u_ps[:], w1_source[:, d, block(m)], hs_bf[:, d, chunk(g)],
+                        start=(d == 0), stop=False,
+                    )
+                for d in range(HB):
+                    nc.tensor.matmul(
+                        u_ps[:], w1_edge[:, d, block(m)], e_bf[:, d, chunk(g)],
+                        start=False, stop=(d == HB - 1),
+                    )
+                u_f32 = ring.tile([P, DEG, NODES], F32, name="u_f32")
+                nc.vector.tensor_tensor(
+                    u_f32[:],
+                    u_ps[:].rearrange("p (i k) -> p k i", k=DEG),
+                    target[:, m, chunk(g, NODES)].unsqueeze(1).to_broadcast([P, DEG, NODES]),
+                    ADD,
+                )
+                nc.scalar.activation(
+                    relu_bf[g // DEG][:, m, :, chunk(g % DEG, NODES)], u_f32[:], RELU
+                )
+
+        for g in range(S // COLS):
+            for m in range(HB):
+                out_ps = psum.tile([P, COLS], F32, tag="bank")
+                for d in range(HB):
+                    for k in range(DEG):
+                        nc.tensor.matmul(
+                            out_ps[:], w_m2_sb[:, d, block(m)], relu_bf[g][:, d, k, :],
+                            start=(d == 0 and k == 0), stop=(d == HB - 1 and k == DEG - 1),
+                        )
+                out_sb = ring.tile([P, COLS], F32, name="out_sb")
+                nc.vector.scalar_tensor_tensor(
+                    out_sb[:], out_ps[:], b_out[:, m : m + 1], h_f32[:, m, chunk(g)], ADD, ADD
+                )
+                nc.sync.dma_start(out[block(m), chunk(g)], out_sb[:])

@@ -64,7 +64,7 @@ def tile_messagepassing_b_kernel(
             for bias_sb, bias in ((b_m1_sb, b_m1), (b_edge_sb, b_edge), (b_m2_sb, b_m2)):
                 nc.gpsimd.dma_start(bias_sb[:], bias.rearrange("(m p) o -> p (m o)", p=P))
         b_out = held.tile([P, HB], F32, name="b_out")
-        nc.vector.tensor_scalar_mul(b_out[:], b_m2_sb[:], float(DEG))
+        nc.gpsimd.tensor_scalar_mul(b_out[:], b_m2_sb[:], float(DEG))
 
         h_f32 = held.tile([P, HB, S], F32, name="h_f32")
         h_bf = held.tile([P, HB, S], BF16, name="h_bf")
@@ -78,10 +78,11 @@ def tile_messagepassing_b_kernel(
                 h_ps = psum.tile([P, COLS], F32, tag="bank")
                 nc.tensor.matmul(h_ps[:], w_node_sb[:, block(m)], x_sb[:, chunk(g)])
                 if m % 2 == 0:
+                    nc.vector.tensor_copy(h_bf[:, m, chunk(g)], h_ps[:])
                     nc.vector.tensor_copy(h_f32[:, m, chunk(g)], h_ps[:])
                 else:
+                    nc.scalar.copy(h_bf[:, m, chunk(g)], h_ps[:])
                     nc.scalar.copy(h_f32[:, m, chunk(g)], h_ps[:])
-                nc.gpsimd.tensor_copy(h_bf[:, m, chunk(g)], h_f32[:, m, chunk(g)])
 
         for g in range(N // COLS):
             looked_up = x_sb[:].indirect(offsets[:, chunk(g, COLS // 16)])

@@ -14,6 +14,7 @@ HB = H // P
 EB = FE // P
 NODES = COLS // DEG
 PSUM_BANKS = 8
+WARM_UP_MATMULS = 6
 
 FLOPS = 2 * (FN * H * S + FN * H * N + FE * H * N + H * H * S + 2 * H * H * N + H * H * N)
 
@@ -35,6 +36,12 @@ def tile_messagepassing_b_kernel(
         tc.tile_pool(name="ring", bufs=4) as ring,
         tc.psum_pool(name="psum", bufs=PSUM_BANKS) as psum,
     ):
+        zeros = held.tile([P, COLS], BF16, name="zeros")
+        nc.vector.memset(zeros[:], 0.0)
+        warm_ps = psum.tile([P, COLS], F32, tag="bank")
+        for i in range(WARM_UP_MATMULS):
+            nc.tensor.matmul(warm_ps[:], zeros[:, block(0)], zeros[:])
+
         x_sb = held.tile([P, S], BF16, name="x_sb")
         nc.sync.dma_start(x_sb[:], x)
         w_node_sb = held.tile([P, H], BF16, name="w_node_sb")

@@ -14,7 +14,6 @@ HB = H // P
 EB = FE // P
 NODES = COLS // DEG
 PSUM_BANKS = 8
-WARM_UP_MATMULS = 6
 
 FLOPS = 2 * (FN * H * S + FN * H * N + FE * H * N + H * H * S + 2 * H * H * N + H * H * N)
 
@@ -36,12 +35,6 @@ def tile_messagepassing_b_kernel(
         tc.tile_pool(name="ring", bufs=4) as ring,
         tc.psum_pool(name="psum", bufs=PSUM_BANKS) as psum,
     ):
-        zeros = held.tile([P, COLS], BF16, name="zeros")
-        nc.vector.memset(zeros[:], 0.0)
-        warm_ps = psum.tile([P, COLS], F32, tag="bank")
-        for i in range(WARM_UP_MATMULS):
-            nc.tensor.matmul(warm_ps[:], zeros[:, block(0)], zeros[:])
-
         x_sb = held.tile([P, S], BF16, name="x_sb")
         nc.sync.dma_start(x_sb[:], x)
         w_node_sb = held.tile([P, H], BF16, name="w_node_sb")
@@ -80,6 +73,16 @@ def tile_messagepassing_b_kernel(
         e_bf = held.tile([P, HB, N], BF16, name="e_bf")
         relu_bf = [held.tile([P, HB, DEG, COLS], BF16, name=f"relu_bf{g}") for g in range(S // COLS)]
 
+        for g in range(N // COLS):
+            looked_up = x_sb[:].indirect(offsets[:, chunk(g, COLS // 16)])
+            for m in range(HB):
+                hs_ps = psum.tile([P, COLS], F32, tag="bank")
+                nc.tensor.matmul(hs_ps[:], w_node_sb[:, block(m)], looked_up)
+                if m % 2 == 0:
+                    nc.vector.tensor_copy(hs_bf[:, m, chunk(g)], hs_ps[:])
+                else:
+                    nc.scalar.copy(hs_bf[:, m, chunk(g)], hs_ps[:])
+
         for g in range(S // COLS):
             for m in range(HB):
                 h_ps = psum.tile([P, COLS], F32, tag="bank")
@@ -90,16 +93,6 @@ def tile_messagepassing_b_kernel(
                 else:
                     nc.scalar.copy(h_bf[:, m, chunk(g)], h_ps[:])
                     nc.scalar.copy(h_f32[:, m, chunk(g)], h_ps[:])
-
-        for g in range(N // COLS):
-            looked_up = x_sb[:].indirect(offsets[:, chunk(g, COLS // 16)])
-            for m in range(HB):
-                hs_ps = psum.tile([P, COLS], F32, tag="bank")
-                nc.tensor.matmul(hs_ps[:], w_node_sb[:, block(m)], looked_up)
-                if m % 2 == 0:
-                    nc.vector.tensor_copy(hs_bf[:, m, chunk(g)], hs_ps[:])
-                else:
-                    nc.scalar.copy(hs_bf[:, m, chunk(g)], hs_ps[:])
 
         for g in range(S // COLS):
             for m in range(HB):

@@ -14,6 +14,7 @@ HB = H // P
 EB = FE // P
 NODES = COLS // DEG
 PSUM_BANKS = 8
+TAIL_PIECES = 4
 
 FLOPS = 2 * (FN * H * S + FN * H * N + FE * H * N + H * H * S + 2 * H * H * N + H * H * N)
 
@@ -43,13 +44,14 @@ def tile_messagepassing_b_kernel(
         nc.sync.dma_start(offsets[:], offs)
 
         w_m1_blocks = w_m1.rearrange("(part d p) c -> part p d c", part=3, p=P)
-        w1_target = held.tile([P, HB, H], BF16, name="w1_target")
-        nc.sync.dma_start(w1_target[:], w_m1_blocks[0])
         w_edge_sb = held.tile([P, EB, H], BF16, name="w_edge_sb")
         nc.sync.dma_start(w_edge_sb[:], w_edge.rearrange("(q p) c -> p q c", p=P))
         ea_sb = held.tile([P, EB, N], BF16, name="ea_sb")
-        for q in range(EB):
-            nc.sync.dma_start(ea_sb[:, q, :], ea[block(q), :])
+        ea_blocks = ea.rearrange("(q p) j -> p q j", p=P)
+        for g in range(N // COLS):
+            nc.sync.dma_start(ea_sb[:, :, chunk(g)], ea_blocks[:, :, chunk(g)])
+        w1_target = held.tile([P, HB, H], BF16, name="w1_target")
+        nc.sync.dma_start(w1_target[:], w_m1_blocks[0])
         w1_source = held.tile([P, HB, H], BF16, name="w1_source")
         nc.sync.dma_start(w1_source[:], w_m1_blocks[1])
         w1_edge = held.tile([P, HB, H], BF16, name="w1_edge")
@@ -72,6 +74,7 @@ def tile_messagepassing_b_kernel(
         target = held.tile([P, HB, S], F32, name="target")
         e_bf = held.tile([P, HB, N], BF16, name="e_bf")
         relu_bf = [held.tile([P, HB, DEG, COLS], BF16, name=f"relu_bf{g}") for g in range(S // COLS)]
+        out_sb = held.tile([P, HB, S], F32, name="out_sb")
 
         for g in range(N // COLS):
             looked_up = x_sb[:].indirect(offsets[:, chunk(g, COLS // 16)])
@@ -94,16 +97,6 @@ def tile_messagepassing_b_kernel(
                     nc.scalar.copy(h_bf[:, m, chunk(g)], h_ps[:])
                     nc.scalar.copy(h_f32[:, m, chunk(g)], h_ps[:])
 
-        for g in range(S // COLS):
-            for m in range(HB):
-                target_ps = psum.tile([P, COLS], F32, tag="bank")
-                for d in range(HB):
-                    nc.tensor.matmul(
-                        target_ps[:], w1_target[:, d, block(m)], h_bf[:, d, chunk(g)],
-                        start=(d == 0), stop=(d == HB - 1),
-                    )
-                nc.vector.tensor_scalar_add(target[:, m, chunk(g)], target_ps[:], b_m1_sb[:, m : m + 1])
-
         for g in range(N // COLS):
             for m in range(HB):
                 e_ps = psum.tile([P, COLS], F32, tag="bank")
@@ -113,6 +106,16 @@ def tile_messagepassing_b_kernel(
                         start=(q == 0), stop=(q == EB - 1),
                     )
                 nc.scalar.activation(e_bf[:, m, chunk(g)], e_ps[:], IDENTITY, bias=b_edge_sb[:, m : m + 1])
+
+        for g in range(S // COLS):
+            for m in range(HB):
+                target_ps = psum.tile([P, COLS], F32, tag="bank")
+                for d in range(HB):
+                    nc.tensor.matmul(
+                        target_ps[:], w1_target[:, d, block(m)], h_bf[:, d, chunk(g)],
+                        start=(d == 0), stop=(d == HB - 1),
+                    )
+                nc.vector.tensor_scalar_add(target[:, m, chunk(g)], target_ps[:], b_m1_sb[:, m : m + 1])
 
         for g in range(N // COLS):
             for m in range(HB):
@@ -140,15 +143,18 @@ def tile_messagepassing_b_kernel(
 
         for g in range(S // COLS):
             for m in range(HB):
-                out_ps = psum.tile([P, COLS], F32, tag="bank")
-                for d in range(HB):
-                    for k in range(DEG):
-                        nc.tensor.matmul(
-                            out_ps[:], w_m2_sb[:, d, block(m)], relu_bf[g][:, d, k, :],
-                            start=(d == 0 and k == 0), stop=(d == HB - 1 and k == DEG - 1),
-                        )
-                out_sb = ring.tile([P, COLS], F32, name="out_sb")
-                nc.vector.scalar_tensor_tensor(
-                    out_sb[:], out_ps[:], b_out[:, m : m + 1], h_f32[:, m, chunk(g)], ADD, ADD
-                )
-                nc.sync.dma_start(out[block(m), chunk(g)], out_sb[:])
+                is_last_block = g == S // COLS - 1 and m == HB - 1
+                width = COLS // TAIL_PIECES if is_last_block else COLS
+                for piece in range(COLS // width):
+                    out_ps = psum.tile([P, width], F32, tag="bank")
+                    for d in range(HB):
+                        for k in range(DEG):
+                            nc.tensor.matmul(
+                                out_ps[:], w_m2_sb[:, d, block(m)], relu_bf[g][:, d, k, chunk(piece, width)],
+                                start=(d == 0 and k == 0), stop=(d == HB - 1 and k == DEG - 1),
+                            )
+                    nodes = slice(g * COLS + piece * width, g * COLS + (piece + 1) * width)
+                    nc.vector.scalar_tensor_tensor(
+                        out_sb[:, m, nodes], out_ps[:], b_out[:, m : m + 1], h_f32[:, m, nodes], ADD, ADD
+                    )
+                    nc.sync.dma_start(out[block(m), nodes], out_sb[:, m, nodes])

@@ -91,11 +91,10 @@ def tile_messagepassing_b_kernel(
                 h_ps = psum.tile([P, COLS], F32, tag="bank")
                 nc.tensor.matmul(h_ps[:], w_node_sb[:, block(m)], x_sb[:, chunk(g)])
                 if m % 2 == 0:
-                    nc.vector.tensor_copy(h_bf[:, m, chunk(g)], h_ps[:])
                     nc.vector.tensor_copy(h_f32[:, m, chunk(g)], h_ps[:])
                 else:
-                    nc.scalar.copy(h_bf[:, m, chunk(g)], h_ps[:])
                     nc.scalar.copy(h_f32[:, m, chunk(g)], h_ps[:])
+                nc.gpsimd.tensor_copy(h_bf[:, m, chunk(g)], h_f32[:, m, chunk(g)])
 
         for g in range(N // COLS):
             for m in range(HB):

@@ -39,9 +39,10 @@ def tile_messagepassing_b_kernel(
         x_sb = held.tile([P, S], BF16, name="x_sb")
         nc.sync.dma_start(x_sb[:], x)
         w_node_sb = held.tile([P, H], BF16, name="w_node_sb")
-        nc.scalar.dma_start(w_node_sb[:], w_node)
+        nc.scalar.dma_start(w_node_sb[:, block(0)], w_node[:, block(0)])
         offsets = held.tile([P, N // 16], U16, name="offsets")
         nc.sync.dma_start(offsets[:], offs)
+        nc.sync.dma_start(w_node_sb[:, P:], w_node[:, P:])
 
         w_m1_blocks = w_m1.rearrange("(part d p) c -> part p d c", part=3, p=P)
         w_edge_sb = held.tile([P, EB, H], BF16, name="w_edge_sb")

@@ -44,6 +44,12 @@ def tile_messagepassing_b_kernel(
         nc.sync.dma_start(offsets[:], offs)
         nc.sync.dma_start(w_node_sb[:, P:], w_node[:, P:])
 
+        def load_bias(bias, name):
+            bias_sb = held.tile([P, HB], F32, name=name)
+            with nc.allow_non_contiguous_dma(reason="a bias has one 4-byte value for each partition"):
+                nc.sync.dma_start(bias_sb[:], bias.rearrange("(m p) o -> p (m o)", p=P))
+            return bias_sb
+
         w_m1_blocks = w_m1.rearrange("(part d p) c -> part p d c", part=3, p=P)
         w_edge_sb = held.tile([P, EB, H], BF16, name="w_edge_sb")
         nc.sync.dma_start(w_edge_sb[:], w_edge.rearrange("(q p) c -> p q c", p=P))
@@ -51,6 +57,8 @@ def tile_messagepassing_b_kernel(
         ea_blocks = ea.rearrange("(q p) j -> p q j", p=P)
         for g in range(N // COLS):
             nc.sync.dma_start(ea_sb[:, :, chunk(g)], ea_blocks[:, :, chunk(g)])
+            if g == 0:
+                b_edge_sb = load_bias(b_edge, "b_edge_sb")
         w1_target = held.tile([P, HB, H], BF16, name="w1_target")
         nc.sync.dma_start(w1_target[:], w_m1_blocks[0])
         w1_source = held.tile([P, HB, H], BF16, name="w1_source")
@@ -60,14 +68,8 @@ def tile_messagepassing_b_kernel(
         w_m2_sb = held.tile([P, HB, H], BF16, name="w_m2_sb")
         nc.sync.dma_start(w_m2_sb[:], w_m2.rearrange("(d p) c -> p d c", p=P))
 
-        b_m1_sb = held.tile([P, HB], F32, name="b_m1_sb")
-        b_edge_sb = held.tile([P, HB], F32, name="b_edge_sb")
-        b_m2_sb = held.tile([P, HB], F32, name="b_m2_sb")
-        with nc.allow_non_contiguous_dma(reason="a bias has one 4-byte value for each partition"):
-            for bias_sb, bias in ((b_m1_sb, b_m1), (b_edge_sb, b_edge), (b_m2_sb, b_m2)):
-                nc.gpsimd.dma_start(bias_sb[:], bias.rearrange("(m p) o -> p (m o)", p=P))
-        b_out = held.tile([P, HB], F32, name="b_out")
-        nc.gpsimd.tensor_scalar_mul(b_out[:], b_m2_sb[:], float(DEG))
+        b_m1_sb = load_bias(b_m1, "b_m1_sb")
+        b_m2_sb = load_bias(b_m2, "b_m2_sb")
 
         h_f32 = held.tile([P, HB, S], F32, name="h_f32")
         h_bf = held.tile([P, HB, S], BF16, name="h_bf")
@@ -140,6 +142,9 @@ def tile_messagepassing_b_kernel(
                 nc.scalar.activation(
                     relu_bf[g // DEG][:, m, :, chunk(g % DEG, NODES)], u_f32[:], RELU
                 )
+
+        b_out = held.tile([P, HB], F32, name="b_out")
+        nc.gpsimd.tensor_scalar_mul(b_out[:], b_m2_sb[:], float(DEG))
 
         for g in range(S // COLS):
             for m in range(HB):

@@ -79,12 +79,12 @@ def tile_messagepassing_b_kernel(
         relu_bf = [held.tile([P, HB, DEG, COLS], BF16, name=f"relu_bf{g}") for g in range(S // COLS)]
         out_sb = held.tile([P, HB, S], F32, name="out_sb")
 
-        for g in range(N // COLS):
-            looked_up = x_sb[:].indirect(offsets[:, chunk(g, COLS // 16)])
-            for m in range(HB):
+        for m in range(HB):
+            for g in range(N // COLS):
+                looked_up = x_sb[:].indirect(offsets[:, chunk(g, COLS // 16)])
                 hs_ps = psum.tile([P, COLS], F32, tag="bank")
                 nc.tensor.matmul(hs_ps[:], w_node_sb[:, block(m)], looked_up)
-                if m % 2 == 0:
+                if g % 2 == 0:
                     nc.vector.tensor_copy(hs_bf[:, m, chunk(g)], hs_ps[:])
                 else:
                     nc.scalar.copy(hs_bf[:, m, chunk(g)], hs_ps[:])

@@ -79,15 +79,18 @@ def tile_messagepassing_b_kernel(
         relu_bf = [held.tile([P, HB, DEG, COLS], BF16, name=f"relu_bf{g}") for g in range(S // COLS)]
         out_sb = held.tile([P, HB, S], F32, name="out_sb")
 
-        for m in range(HB):
-            for g in range(N // COLS):
-                looked_up = x_sb[:].indirect(offsets[:, chunk(g, COLS // 16)])
-                hs_ps = psum.tile([P, COLS], F32, tag="bank")
-                nc.tensor.matmul(hs_ps[:], w_node_sb[:, block(m)], looked_up)
-                if g % 2 == 0:
-                    nc.vector.tensor_copy(hs_bf[:, m, chunk(g)], hs_ps[:])
-                else:
-                    nc.scalar.copy(hs_bf[:, m, chunk(g)], hs_ps[:])
+        def source_nodes(ms):
+            for m in ms:
+                for g in range(N // COLS):
+                    looked_up = x_sb[:].indirect(offsets[:, chunk(g, COLS // 16)])
+                    hs_ps = psum.tile([P, COLS], F32, tag="bank")
+                    nc.tensor.matmul(hs_ps[:], w_node_sb[:, block(m)], looked_up)
+                    if g % 2 == 0:
+                        nc.vector.tensor_copy(hs_bf[:, m, chunk(g)], hs_ps[:])
+                    else:
+                        nc.scalar.copy(hs_bf[:, m, chunk(g)], hs_ps[:])
+
+        source_nodes(range(HB // 2))
 
         for g in range(S // COLS):
             for m in range(HB):
@@ -108,6 +111,8 @@ def tile_messagepassing_b_kernel(
                         start=(q == 0), stop=(q == EB - 1),
                     )
                 nc.scalar.activation(e_bf[:, m, chunk(g)], e_ps[:], IDENTITY, bias=b_edge_sb[:, m : m + 1])
+
+        source_nodes(range(HB // 2, HB))
 
         for g in range(S // COLS):
             for m in range(HB):

@@ -100,7 +100,9 @@ def tile_messagepassing_b_kernel(
                     nc.vector.tensor_copy(h_f32[:, m, chunk(g)], h_ps[:])
                 else:
                     nc.scalar.copy(h_f32[:, m, chunk(g)], h_ps[:])
-                nc.gpsimd.tensor_copy(h_bf[:, m, chunk(g)], h_f32[:, m, chunk(g)])
+        for g in range(S // COLS):
+            for m in range(HB):
+                nc.vector.tensor_copy(h_bf[:, m, chunk(g)], h_f32[:, m, chunk(g)])
 
         for g in range(N // COLS):
             for m in range(HB):
@@ -149,7 +151,7 @@ def tile_messagepassing_b_kernel(
                 )
 
         b_out = held.tile([P, HB], F32, name="b_out")
-        nc.gpsimd.tensor_scalar_mul(b_out[:], b_m2_sb[:], float(DEG))
+        nc.vector.tensor_scalar_mul(b_out[:], b_m2_sb[:], float(DEG))
 
         for g in range(S // COLS):
             for m in range(HB):

import concourse.mybir as mybir

BF16, F32, U16 = mybir.dt.bfloat16, mybir.dt.float32, mybir.dt.uint16
ADD = mybir.AluOpType.add
IDENTITY = mybir.ActivationFunctionType.Identity
RELU = mybir.ActivationFunctionType.Relu

P = 128
FN, FE, H = 128, 1024, 512
S, N = 1024, 2048
DEG = N // S
COLS = 512
HB = H // P
EB = FE // P
NODES = COLS // DEG
PSUM_BANKS = 8
TAIL_PIECES = 4

FLOPS = 2 * (FN * H * S + FN * H * N + FE * H * N + H * H * S + 2 * H * H * N + H * H * N)


def block(b):
    return slice(b * P, (b + 1) * P)


def chunk(i, width=COLS):
    return slice(i * width, (i + 1) * width)


def tile_messagepassing_b_kernel(
    tc, x, ea, w_node, w_edge, b_edge, w_m1, b_m1, w_m2, b_m2, offs, out
):
    nc = tc.nc
    with (
        tc.tile_pool(name="held", bufs=1) as held,
        tc.tile_pool(name="ring", bufs=4) as ring,
        tc.psum_pool(name="psum", bufs=PSUM_BANKS) as psum,
    ):
        x_sb = held.tile([P, S], BF16, name="x_sb")
        nc.sync.dma_start(x_sb[:], x)
        w_node_sb = held.tile([P, H], BF16, name="w_node_sb")
        nc.scalar.dma_start(w_node_sb[:, block(0)], w_node[:, block(0)])
        offsets = held.tile([P, N // 16], U16, name="offsets")
        nc.sync.dma_start(offsets[:], offs)
        nc.sync.dma_start(w_node_sb[:, P:], w_node[:, P:])

        def load_bias(bias, name):
            bias_sb = held.tile([P, HB], F32, name=name)
            with nc.allow_non_contiguous_dma(reason="a bias has one 4-byte value for each partition"):
                nc.sync.dma_start(bias_sb[:], bias.rearrange("(m p) o -> p (m o)", p=P))
            return bias_sb

        w_m1_blocks = w_m1.rearrange("(part d p) c -> part p d c", part=3, p=P)
        w_edge_sb = held.tile([P, EB, H], BF16, name="w_edge_sb")
        nc.sync.dma_start(w_edge_sb[:], w_edge.rearrange("(q p) c -> p q c", p=P))
        ea_sb = held.tile([P, EB, N], BF16, name="ea_sb")
        ea_blocks = ea.rearrange("(q p) j -> p q j", p=P)
        for g in range(N // COLS):
            nc.sync.dma_start(ea_sb[:, :, chunk(g)], ea_blocks[:, :, chunk(g)])
            if g == 0:
                b_edge_sb = load_bias(b_edge, "b_edge_sb")
        w1_target = held.tile([P, HB, H], BF16, name="w1_target")
        nc.sync.dma_start(w1_target[:], w_m1_blocks[0])
        w1_source = held.tile([P, HB, H], BF16, name="w1_source")
        nc.sync.dma_start(w1_source[:], w_m1_blocks[1])
        w1_edge = held.tile([P, HB, H], BF16, name="w1_edge")
        nc.sync.dma_start(w1_edge[:], w_m1_blocks[2])
        w_m2_sb = held.tile([P, HB, H], BF16, name="w_m2_sb")
        nc.sync.dma_start(w_m2_sb[:], w_m2.rearrange("(d p) c -> p d c", p=P))

        b_m1_sb = load_bias(b_m1, "b_m1_sb")
        b_m2_sb = load_bias(b_m2, "b_m2_sb")

        h_f32 = held.tile([P, HB, S], F32, name="h_f32")
        h_bf = held.tile([P, HB, S], BF16, name="h_bf")
        hs_bf = held.tile([P, HB, N], BF16, name="hs_bf")
        target = held.tile([P, HB, S], F32, name="target")
        e_bf = held.tile([P, HB, N], BF16, name="e_bf")
        relu_bf = [held.tile([P, HB, DEG, COLS], BF16, name=f"relu_bf{g}") for g in range(S // COLS)]
        out_sb = held.tile([P, HB, S], F32, name="out_sb")

        def source_nodes(ms):
            for m in ms:
                for g in range(N // COLS):
                    looked_up = x_sb[:].indirect(offsets[:, chunk(g, COLS // 16)])
                    hs_ps = psum.tile([P, COLS], F32, tag="bank")
                    nc.tensor.matmul(hs_ps[:], w_node_sb[:, block(m)], looked_up)
                    if g % 2 == 0:
                        nc.vector.tensor_copy(hs_bf[:, m, chunk(g)], hs_ps[:])
                    else:
                        nc.scalar.copy(hs_bf[:, m, chunk(g)], hs_ps[:])

        source_nodes(range(HB // 2))

        for g in range(S // COLS):
            for m in range(HB):
                h_ps = psum.tile([P, COLS], F32, tag="bank")
                nc.tensor.matmul(h_ps[:], w_node_sb[:, block(m)], x_sb[:, chunk(g)])
                if m % 2 == 0:
                    nc.vector.tensor_copy(h_f32[:, m, chunk(g)], h_ps[:])
                else:
                    nc.scalar.copy(h_f32[:, m, chunk(g)], h_ps[:])
        for g in range(S // COLS):
            for m in range(HB):
                nc.vector.tensor_copy(h_bf[:, m, chunk(g)], h_f32[:, m, chunk(g)])

        for g in range(N // COLS):
            for m in range(HB):
                e_ps = psum.tile([P, COLS], F32, tag="bank")
                for q in range(EB):
                    nc.tensor.matmul(
                        e_ps[:], w_edge_sb[:, q, block(m)], ea_sb[:, q, chunk(g)],
                        start=(q == 0), stop=(q == EB - 1),
                    )
                nc.scalar.activation(e_bf[:, m, chunk(g)], e_ps[:], IDENTITY, bias=b_edge_sb[:, m : m + 1])

        source_nodes(range(HB // 2, HB))

        for g in range(S // COLS):
            for m in range(HB):
                target_ps = psum.tile([P, COLS], F32, tag="bank")
                for d in range(HB):
                    nc.tensor.matmul(
                        target_ps[:], w1_target[:, d, block(m)], h_bf[:, d, chunk(g)],
                        start=(d == 0), stop=(d == HB - 1),
                    )
                nc.vector.tensor_scalar_add(target[:, m, chunk(g)], target_ps[:], b_m1_sb[:, m : m + 1])

        for g in range(N // COLS):
            for m in range(HB):
                u_ps = psum.tile([P, COLS], F32, tag="bank")
                for d in range(HB):
                    nc.tensor.matmul(
                        u_ps[:], w1_source[:, d, block(m)], hs_bf[:, d, chunk(g)],
                        start=(d == 0), stop=False,
                    )
                for d in range(HB):
                    nc.tensor.matmul(
                        u_ps[:], w1_edge[:, d, block(m)], e_bf[:, d, chunk(g)],
                        start=False, stop=(d == HB - 1),
                    )
                u_f32 = ring.tile([P, DEG, NODES], F32, name="u_f32")
                nc.vector.tensor_tensor(
                    u_f32[:],
                    u_ps[:].rearrange("p (i k) -> p k i", k=DEG),
                    target[:, m, chunk(g, NODES)].unsqueeze(1).to_broadcast([P, DEG, NODES]),
                    ADD,
                )
                nc.scalar.activation(
                    relu_bf[g // DEG][:, m, :, chunk(g % DEG, NODES)], u_f32[:], RELU
                )

        b_out = held.tile([P, HB], F32, name="b_out")
        nc.vector.tensor_scalar_mul(b_out[:], b_m2_sb[:], float(DEG))

        for g in range(S // COLS):
            for m in range(HB):
                is_last_block = g == S // COLS - 1 and m == HB - 1
                width = COLS // TAIL_PIECES if is_last_block else COLS
                for piece in range(COLS // width):
                    out_ps = psum.tile([P, width], F32, tag="bank")
                    for d in range(HB):
                        for k in range(DEG):
                            nc.tensor.matmul(
                                out_ps[:], w_m2_sb[:, d, block(m)], relu_bf[g][:, d, k, chunk(piece, width)],
                                start=(d == 0 and k == 0), stop=(d == HB - 1 and k == DEG - 1),
                            )
                    nodes = slice(g * COLS + piece * width, g * COLS + (piece + 1) * width)
                    nc.vector.scalar_tensor_tensor(
                        out_sb[:, m, nodes], out_ps[:], b_out[:, m : m + 1], h_f32[:, m, nodes], ADD, ADD
                    )
                    nc.sync.dma_start(out[block(m), nodes], out_sb[:, m, nodes])
